import numpy as np
import ml_dtypes


def mxq(x, axis, fmt="e4m3"):
    dtype, down = {"e4m3": (ml_dtypes.float8_e4m3fn, 7), "e5m2": (ml_dtypes.float8_e5m2, 14)}[fmt]
    v = np.moveaxis(np.asarray(x, np.float32).astype(ml_dtypes.bfloat16).astype(np.float64), axis, -1)
    blocks = v.reshape(v.shape[:-1] + (-1, 32))
    amax = np.abs(blocks).max(-1, keepdims=True)
    byte = np.maximum(np.where(amax > 0, np.frexp(amax)[1] - 1 + 127, 0) - down, 1)
    scale = np.exp2(byte - 127.0)
    codes = (blocks / scale).astype(np.float32).astype(dtype).astype(np.float64)
    return np.moveaxis((codes * scale).reshape(v.shape), -1, axis)


WIDE = False


def mx_kscale(k):
    if not WIDE:
        return np.ones(k)
    levels = np.array([10, -10, 5, -5, 0])
    a = np.random.permutation(np.resize(levels, k // 512 * 4)).reshape(k // 512, 4)
    idx = np.arange(k)
    return np.exp2(a[idx // 512, idx % 128 // 32])


BF16 = ml_dtypes.bfloat16


def bf(x):
    return np.asarray(x, np.float32).astype(BF16)


def f64(x):
    return np.asarray(x).astype(np.float64)


B, C, N, T, E, O, KCH, ORD = 8, 64, 512, 12, 10, 64, 3, 2
SIG = 3.0


def setup_inputs():
    s = mx_kscale(N)
    w = np.exp(SIG * np.random.standard_normal((N, N)))
    adj = w / w.sum(-1, keepdims=True)
    return {"x": bf(np.random.standard_normal((B, C, N, T)) / s[None, None, :, None]),
            "adj": bf(adj * s[:, None] / s[None, :])}


def reference(x, adj):
    R = B * C * T
    xr = f64(x).transpose(0, 1, 3, 2).reshape(R, N)
    aq = mxq(f64(adj), 0, "e4m3")
    x1 = mxq(xr, 1, "e4m3") @ aq
    x2 = mxq(x1, 1, "e4m3") @ aq
    return (x1.reshape(B, C, T, N).transpose(0, 1, 3, 2), x2.reshape(B, C, T, N).transpose(0, 1, 3, 2))

@@ -1,0 +1,178 @@
+from contextlib import ExitStack
+
+import concourse.mybir as mybir
+from concourse.masks import make_identity
+
+BF16 = mybir.dt.bfloat16
+F32 = mybir.dt.float32
+U32 = mybir.dt.uint32
+U8 = mybir.dt.uint8
+FP8X4 = mybir.dt.float8_e4m3fn_x4
+
+P = 128
+PACK = 4
+NODES = P * PACK
+STEPS = 12
+SERIES = 8 * 64
+BLOCKS = SERIES // P
+QUADS = STEPS // 4
+NODE_TILES = NODES // P
+BANK = 512
+
+FLOPS = 2 * 2 * SERIES * STEPS * NODES * NODES
+
+
+def tile_avwgcn_pb_t_kernel(tc, x, adj, out_0, out_1):
+    nc = tc.nc
+    x_rows = x.rearrange("b c v l -> (b c) (v l)")
+    out_rows = [
+        out_0.rearrange("b c w l -> (b c) (w l)"),
+        out_1.rearrange("b c w l -> (b c) (w l)"),
+    ]
+
+    with ExitStack() as ctx:
+        keep = ctx.enter_context(tc.tile_pool(name="keep", bufs=1))
+        sort_pool = ctx.enter_context(tc.tile_pool(name="sort", bufs=3))
+        group_pool = ctx.enter_context(tc.tile_pool(name="group", bufs=3))
+        hop_pool = ctx.enter_context(tc.tile_pool(name="hop", bufs=6))
+        code_pool = ctx.enter_context(tc.tile_pool(name="codes", bufs=2))
+        out_pool = ctx.enter_context(tc.tile_pool(name="outs", bufs=12))
+        psum_t = ctx.enter_context(tc.psum_pool(name="psum_t", bufs=2))
+        psum_n = ctx.enter_context(tc.psum_pool(name="psum_n", bufs=3))
+        psum_s = ctx.enter_context(tc.psum_pool(name="psum_s", bufs=3))
+
+        adj_raw = keep.tile([P, PACK, NODES], BF16)
+        nc.sync.dma_start(out=adj_raw[:], in_=adj.rearrange("(p j) w -> p j w", j=PACK))
+        x_in = []
+        for g in range(BLOCKS):
+            x_block = keep.tile([P, NODES * STEPS], BF16, name="x_in%d" % g)
+            nc.sync.dma_start(out=x_block[:], in_=x_rows[g * P : (g + 1) * P, :])
+            x_in.append(x_block)
+
+        ident = keep.tile([P, P], F32)
+        make_identity(nc, ident[:])
+
+        adj_nat_grouped = keep.tile([P, NODES, PACK], BF16, align_bytes=64)
+        nc.vector.tensor_copy(out=adj_nat_grouped[:], in_=adj_raw[:].rearrange("p j w -> p w j"))
+        adj_mod_grouped = keep.tile([P, PACK, P, PACK], BF16, align_bytes=64)
+        nc.scalar.copy(
+            out=adj_mod_grouped[:], in_=adj_raw[:].rearrange("p j (m t) -> p t m j", t=PACK)
+        )
+        adj_nat_codes = keep.tile([P, NODES], U32, align_bytes=64)
+        adj_nat_scales = keep.tile([P, NODES], U8, align_bytes=64)
+        nc.vector.quantize_mx(
+            out=adj_nat_codes[:].bitcast(FP8X4),
+            scales=adj_nat_scales[:],
+            in_=adj_nat_grouped[:].rearrange("p w j -> p (w j)"),
+        )
+        adj_mod_codes = keep.tile([P, NODES], U32, align_bytes=64)
+        adj_mod_scales = keep.tile([P, NODES], U8, align_bytes=64)
+        nc.vector.quantize_mx(
+            out=adj_mod_codes[:].bitcast(FP8X4),
+            scales=adj_mod_scales[:],
+            in_=adj_mod_grouped[:].rearrange("p t m j -> p (t m j)"),
+        )
+
+        x_codes = {}
+        x_scales = {}
+        x1_codes = {}
+        x1_scales = {}
+
+        def new_operand(codes, scales, g, name):
+            codes[g] = code_pool.tile([P, STEPS * P], U32, align_bytes=64, name=name + "_codes")
+            scales[g] = code_pool.tile([P, STEPS * P], U8, align_bytes=64, name=name + "_scales")
+
+        def quantise_x(g, q):
+            if q == 0:
+                new_operand(x_codes, x_scales, g, "x")
+            x_sorted = sort_pool.tile([P, 4 * NODES], BF16)
+            src = x_in[g][:].rearrange("p (i u e l) -> p u i e l", u=2, e=2, l=STEPS)
+            dst = x_sorted[:].rearrange("p (l u i e) -> p u i e l", l=4, u=2, e=2)
+            for u in range(2):
+                nc.vector.tensor_copy(out=dst[:, u], in_=src[:, u, :, :, 4 * q : 4 * q + 4])
+            words = x_sorted[:].bitcast(F32)
+
+            x_grouped = group_pool.tile([P, 4 * P * PACK], BF16, align_bytes=64)
+            grouped_words = x_grouped[:].bitcast(F32)
+            for h in range(2):
+                bank = psum_t.tile([P, BANK], F32, name="bank_t")
+                for c in range(4):
+                    nc.tensor.transpose(
+                        bank[:, c * P : (c + 1) * P],
+                        words[:, (4 * h + c) * P : (4 * h + c + 1) * P],
+                        ident[:],
+                    )
+                copy_out = nc.vector.tensor_copy if h == 0 else nc.scalar.copy
+                copy_out(
+                    out=grouped_words[:, h * BANK : (h + 1) * BANK].rearrange(
+                        "p (l s u) -> p l s u", l=2, u=2
+                    ),
+                    in_=bank[:].rearrange("p (l u s) -> p l s u", l=2, u=2),
+                )
+            cols = slice(q * 4 * P, (q + 1) * 4 * P)
+            nc.vector.quantize_mx(
+                out=x_codes[g][:, cols].bitcast(FP8X4), scales=x_scales[g][:, cols], in_=x_grouped[:]
+            )
+
+        def hop1_for_hop2(g, steps):
+            grouped = {}
+            for l in steps:
+                cols = slice(l * P, (l + 1) * P)
+                bank = psum_n.tile([P, PACK, P], F32, name="bank_n")
+                for t in range(PACK):
+                    nc.tensor.matmul_mx(
+                        out=bank[:, t, :],
+                        lhsT=adj_mod_codes[:, t * P : (t + 1) * P].bitcast(FP8X4),
+                        lhsT_scale=adj_mod_scales[:, t * P : (t + 1) * P],
+                        rhs=x_codes[g][:, cols].bitcast(FP8X4),
+                        rhs_scale=x_scales[g][:, cols],
+                        start=True,
+                        stop=True,
+                    )
+                grouped[l] = hop_pool.tile([P, P, PACK], BF16, align_bytes=64, name="x1_grouped")
+                nc.vector.tensor_copy(out=grouped[l][:], in_=bank[:].rearrange("p t s -> p s t"))
+            for l in steps:
+                cols = slice(l * P, (l + 1) * P)
+                nc.vector.quantize_mx(
+                    out=x1_codes[g][:, cols].bitcast(FP8X4),
+                    scales=x1_scales[g][:, cols],
+                    in_=grouped[l][:].rearrange("p s t -> p (s t)"),
+                )
+
+        def hop_to_hbm(hop, codes, scales, g, n):
+            node_cols = slice(n * P, (n + 1) * P)
+            result = out_pool.tile([P, P, STEPS], F32)
+            for q in range(QUADS):
+                bank = psum_s.tile([P, 4, P], F32, name="bank_s")
+                for j in range(4):
+                    cols = slice((4 * q + j) * P, (4 * q + j + 1) * P)
+                    nc.tensor.matmul_mx(
+                        out=bank[:, j, :],
+                        lhsT=codes[g][:, cols].bitcast(FP8X4),
+                        lhsT_scale=scales[g][:, cols],
+                        rhs=adj_nat_codes[:, node_cols].bitcast(FP8X4),
+                        rhs_scale=adj_nat_scales[:, node_cols],
+                        start=True,
+                        stop=True,
+                    )
+                nc.scalar.copy(
+                    out=result[:, :, 4 * q : 4 * q + 4], in_=bank[:].rearrange("p l w -> p w l")
+                )
+            nc.sync.dma_start(
+                out=out_rows[hop][g * P : (g + 1) * P, n * P * STEPS : (n + 1) * P * STEPS],
+                in_=result[:].rearrange("p w l -> p (w l)"),
+            )
+
+        for q in range(QUADS):
+            quantise_x(0, q)
+        for g in range(BLOCKS + 1):
+            if g < BLOCKS:
+                new_operand(x1_codes, x1_scales, g, "x1")
+            for n in range(NODE_TILES):
+                if g < BLOCKS:
+                    hop1_for_hop2(g, range(n * STEPS // NODE_TILES, (n + 1) * STEPS // NODE_TILES))
+                    hop_to_hbm(0, x_codes, x_scales, g, n)
+                if g >= 1:
+                    hop_to_hbm(1, x1_codes, x1_scales, g - 1, n)
+                if g + 1 < BLOCKS and n < QUADS:
+                    quantise_x(g + 1, n)

@@ -32,14 +32,14 @@ def tile_avwgcn_pb_t_kernel(tc, x, adj, out_0, out_1):
 
     with ExitStack() as ctx:
         keep = ctx.enter_context(tc.tile_pool(name="keep", bufs=1))
-        sort_pool = ctx.enter_context(tc.tile_pool(name="sort", bufs=3))
-        group_pool = ctx.enter_context(tc.tile_pool(name="group", bufs=3))
+        sort_pool = ctx.enter_context(tc.tile_pool(name="sort", bufs=6))
+        group_pool = ctx.enter_context(tc.tile_pool(name="group", bufs=4))
         hop_pool = ctx.enter_context(tc.tile_pool(name="hop", bufs=6))
         code_pool = ctx.enter_context(tc.tile_pool(name="codes", bufs=2))
         out_pool = ctx.enter_context(tc.tile_pool(name="outs", bufs=12))
         psum_t = ctx.enter_context(tc.psum_pool(name="psum_t", bufs=2))
-        psum_n = ctx.enter_context(tc.psum_pool(name="psum_n", bufs=3))
-        psum_s = ctx.enter_context(tc.psum_pool(name="psum_s", bufs=3))
+        psum_n = ctx.enter_context(tc.psum_pool(name="psum_n", bufs=2))
+        psum_s = ctx.enter_context(tc.psum_pool(name="psum_s", bufs=4))
 
         adj_raw = keep.tile([P, PACK, NODES], BF16)
         nc.sync.dma_start(out=adj_raw[:], in_=adj.rearrange("(p j) w -> p j w", j=PACK))
@@ -102,8 +102,7 @@ def tile_avwgcn_pb_t_kernel(tc, x, adj, out_0, out_1):
                         words[:, (4 * h + c) * P : (4 * h + c + 1) * P],
                         ident[:],
                     )
-                copy_out = nc.vector.tensor_copy if h == 0 else nc.scalar.copy
-                copy_out(
+                nc.scalar.copy(
                     out=grouped_words[:, h * BANK : (h + 1) * BANK].rearrange(
                         "p (l s u) -> p l s u", l=2, u=2
                     ),
@@ -114,50 +113,50 @@ def tile_avwgcn_pb_t_kernel(tc, x, adj, out_0, out_1):
                 out=x_codes[g][:, cols].bitcast(FP8X4), scales=x_scales[g][:, cols], in_=x_grouped[:]
             )
 
-        def hop1_for_hop2(g, steps):
-            grouped = {}
-            for l in steps:
-                cols = slice(l * P, (l + 1) * P)
-                bank = psum_n.tile([P, PACK, P], F32, name="bank_n")
-                for t in range(PACK):
-                    nc.tensor.matmul_mx(
-                        out=bank[:, t, :],
-                        lhsT=adj_mod_codes[:, t * P : (t + 1) * P].bitcast(FP8X4),
-                        lhsT_scale=adj_mod_scales[:, t * P : (t + 1) * P],
-                        rhs=x_codes[g][:, cols].bitcast(FP8X4),
-                        rhs_scale=x_scales[g][:, cols],
-                        start=True,
-                        stop=True,
-                    )
-                grouped[l] = hop_pool.tile([P, P, PACK], BF16, align_bytes=64, name="x1_grouped")
-                nc.vector.tensor_copy(out=grouped[l][:], in_=bank[:].rearrange("p t s -> p s t"))
-            for l in steps:
-                cols = slice(l * P, (l + 1) * P)
-                nc.vector.quantize_mx(
-                    out=x1_codes[g][:, cols].bitcast(FP8X4),
-                    scales=x1_scales[g][:, cols],
-                    in_=grouped[l][:].rearrange("p s t -> p (s t)"),
+        def node_major_bank(g, l):
+            cols = slice(l * P, (l + 1) * P)
+            bank = psum_n.tile([P, PACK, P], F32, name="bank_n")
+            for t in range(PACK):
+                nc.tensor.matmul_mx(
+                    out=bank[:, t, :],
+                    lhsT=adj_mod_codes[:, t * P : (t + 1) * P].bitcast(FP8X4),
+                    lhsT_scale=adj_mod_scales[:, t * P : (t + 1) * P],
+                    rhs=x_codes[g][:, cols].bitcast(FP8X4),
+                    rhs_scale=x_scales[g][:, cols],
+                    start=True,
+                    stop=True,
                 )
+            x1_grouped = hop_pool.tile([P, P, PACK], BF16, align_bytes=64)
+            copy_out = nc.vector.tensor_copy if l % 4 == 3 else nc.scalar.copy
+            copy_out(out=x1_grouped[:], in_=bank[:].rearrange("p t s -> p s t"))
+            return x1_grouped
 
-        def hop_to_hbm(hop, codes, scales, g, n):
+        def quantise_x1(g, l, x1_grouped):
+            cols = slice(l * P, (l + 1) * P)
+            nc.vector.quantize_mx(
+                out=x1_codes[g][:, cols].bitcast(FP8X4),
+                scales=x1_scales[g][:, cols],
+                in_=x1_grouped[:].rearrange("p s t -> p (s t)"),
+            )
+
+        def series_major_bank(result, hop, codes, scales, n, q):
             node_cols = slice(n * P, (n + 1) * P)
-            result = out_pool.tile([P, P, STEPS], F32)
-            for q in range(QUADS):
-                bank = psum_s.tile([P, 4, P], F32, name="bank_s")
-                for j in range(4):
-                    cols = slice((4 * q + j) * P, (4 * q + j + 1) * P)
-                    nc.tensor.matmul_mx(
-                        out=bank[:, j, :],
-                        lhsT=codes[g][:, cols].bitcast(FP8X4),
-                        lhsT_scale=scales[g][:, cols],
-                        rhs=adj_nat_codes[:, node_cols].bitcast(FP8X4),
-                        rhs_scale=adj_nat_scales[:, node_cols],
-                        start=True,
-                        stop=True,
-                    )
-                nc.scalar.copy(
-                    out=result[:, :, 4 * q : 4 * q + 4], in_=bank[:].rearrange("p l w -> p w l")
+            bank = psum_s.tile([P, 4, P], F32, name="bank_s")
+            for j in range(4):
+                cols = slice((4 * q + j) * P, (4 * q + j + 1) * P)
+                nc.tensor.matmul_mx(
+                    out=bank[:, j, :],
+                    lhsT=codes[:, cols].bitcast(FP8X4),
+                    lhsT_scale=scales[:, cols],
+                    rhs=adj_nat_codes[:, node_cols].bitcast(FP8X4),
+                    rhs_scale=adj_nat_scales[:, node_cols],
+                    start=True,
+                    stop=True,
                 )
+            copy_out = nc.scalar.copy if (hop + n) % 2 == 0 else nc.vector.tensor_copy
+            copy_out(out=result[:, :, 4 * q : 4 * q + 4], in_=bank[:].rearrange("p l w -> p w l"))
+
+        def store(hop, g, n, result):
             nc.sync.dma_start(
                 out=out_rows[hop][g * P : (g + 1) * P, n * P * STEPS : (n + 1) * P * STEPS],
                 in_=result[:].rearrange("p w l -> p (w l)"),
@@ -166,13 +165,28 @@ def tile_avwgcn_pb_t_kernel(tc, x, adj, out_0, out_1):
         for q in range(QUADS):
             quantise_x(0, q)
         for g in range(BLOCKS + 1):
-            if g < BLOCKS:
+            first_hop = g < BLOCKS
+            second_hop = g >= 1
+            if first_hop:
                 new_operand(x1_codes, x1_scales, g, "x1")
             for n in range(NODE_TILES):
-                if g < BLOCKS:
-                    hop1_for_hop2(g, range(n * STEPS // NODE_TILES, (n + 1) * STEPS // NODE_TILES))
-                    hop_to_hbm(0, x_codes, x_scales, g, n)
-                if g >= 1:
-                    hop_to_hbm(1, x1_codes, x1_scales, g - 1, n)
+                x1_grouped = {}
+                if first_hop:
+                    result_1 = out_pool.tile([P, P, STEPS], F32, tag="result")
+                if second_hop:
+                    result_2 = out_pool.tile([P, P, STEPS], F32, tag="result")
+                for q in range(QUADS):
+                    if first_hop:
+                        l = n * QUADS + q
+                        x1_grouped[l] = node_major_bank(g, l)
+                        series_major_bank(result_1, 0, x_codes[g], x_scales[g], n, q)
+                    if second_hop:
+                        series_major_bank(result_2, 1, x1_codes[g - 1], x1_scales[g - 1], n, q)
+                if first_hop:
+                    store(0, g, n, result_1)
+                if second_hop:
+                    store(1, g - 1, n, result_2)
+                for l in x1_grouped:
+                    quantise_x1(g, l, x1_grouped[l])
                 if g + 1 < BLOCKS and n < QUADS:
                     quantise_x(g + 1, n)

@@ -32,14 +32,15 @@ def tile_avwgcn_pb_t_kernel(tc, x, adj, out_0, out_1):
 
     with ExitStack() as ctx:
         keep = ctx.enter_context(tc.tile_pool(name="keep", bufs=1))
-        sort_pool = ctx.enter_context(tc.tile_pool(name="sort", bufs=6))
-        group_pool = ctx.enter_context(tc.tile_pool(name="group", bufs=4))
+        sort_pool = ctx.enter_context(tc.tile_pool(name="sort", bufs=4))
+        group_pool = ctx.enter_context(tc.tile_pool(name="group", bufs=3))
         hop_pool = ctx.enter_context(tc.tile_pool(name="hop", bufs=6))
         code_pool = ctx.enter_context(tc.tile_pool(name="codes", bufs=2))
         out_pool = ctx.enter_context(tc.tile_pool(name="outs", bufs=12))
         psum_t = ctx.enter_context(tc.psum_pool(name="psum_t", bufs=2))
         psum_n = ctx.enter_context(tc.psum_pool(name="psum_n", bufs=2))
         psum_s = ctx.enter_context(tc.psum_pool(name="psum_s", bufs=4))
+        ctx.enter_context(tc.manual_schedule())
 
         adj_raw = keep.tile([P, PACK, NODES], BF16)
         nc.sync.dma_start(out=adj_raw[:], in_=adj.rearrange("(p j) w -> p j w", j=PACK))
@@ -77,23 +78,38 @@ def tile_avwgcn_pb_t_kernel(tc, x, adj, out_0, out_1):
         x_scales = {}
         x1_codes = {}
         x1_scales = {}
+        x_sorted = {}
+        x_grouped = {}
+        x1_grouped = {}
 
         def new_operand(codes, scales, g, name):
             codes[g] = code_pool.tile([P, STEPS * P], U32, align_bytes=64, name=name + "_codes")
             scales[g] = code_pool.tile([P, STEPS * P], U8, align_bytes=64, name=name + "_scales")
 
-        def quantise_x(g, q):
-            if q == 0:
-                new_operand(x_codes, x_scales, g, "x")
-            x_sorted = sort_pool.tile([P, 4 * NODES], BF16)
+        def sort_x(g, q):
+            x_sorted[g, q] = sort_pool.tile([P, 4 * NODES], BF16, name="x_sorted")
             src = x_in[g][:].rearrange("p (i u e l) -> p u i e l", u=2, e=2, l=STEPS)
-            dst = x_sorted[:].rearrange("p (l u i e) -> p u i e l", l=4, u=2, e=2)
+            dst = x_sorted[g, q][:].rearrange("p (l u i e) -> p u i e l", l=4, u=2, e=2)
             for u in range(2):
-                nc.vector.tensor_copy(out=dst[:, u], in_=src[:, u, :, :, 4 * q : 4 * q + 4])
-            words = x_sorted[:].bitcast(F32)
+                if g == 0:
+                    nc.vector.tensor_copy(out=dst[:, u], in_=src[:, u, :, :, 4 * q : 4 * q + 4])
+                else:
+                    nc.gpsimd.tensor_scalar(
+                        out=dst[:, u],
+                        in0=src[:, u, :, :, 4 * q : 4 * q + 4],
+                        scalar1=1.0,
+                        scalar2=0.0,
+                        op0=mybir.AluOpType.mult,
+                        op1=mybir.AluOpType.add,
+                    )
 
-            x_grouped = group_pool.tile([P, 4 * P * PACK], BF16, align_bytes=64)
-            grouped_words = x_grouped[:].bitcast(F32)
+        def transpose_x(g, q):
+            words = x_sorted[g, q][:].bitcast(F32)
+            x_grouped[g, q] = group_pool.tile(
+                [P, 4 * P * PACK], BF16, align_bytes=64, name="x_grouped"
+            )
+            grouped_words = x_grouped[g, q][:].bitcast(F32)
+            banks = []
             for h in range(2):
                 bank = psum_t.tile([P, BANK], F32, name="bank_t")
                 for c in range(4):
@@ -102,15 +118,24 @@ def tile_avwgcn_pb_t_kernel(tc, x, adj, out_0, out_1):
                         words[:, (4 * h + c) * P : (4 * h + c + 1) * P],
                         ident[:],
                     )
-                nc.scalar.copy(
+                banks.append(bank)
+            for h in range(2):
+                copy_out = nc.vector.tensor_copy if h == 0 else nc.scalar.copy
+                copy_out(
                     out=grouped_words[:, h * BANK : (h + 1) * BANK].rearrange(
                         "p (l s u) -> p l s u", l=2, u=2
                     ),
-                    in_=bank[:].rearrange("p (l u s) -> p l s u", l=2, u=2),
+                    in_=banks[h][:].rearrange("p (l u s) -> p l s u", l=2, u=2),
                 )
+
+        def quantise_x(g, q):
+            if q == 0:
+                new_operand(x_codes, x_scales, g, "x")
             cols = slice(q * 4 * P, (q + 1) * 4 * P)
             nc.vector.quantize_mx(
-                out=x_codes[g][:, cols].bitcast(FP8X4), scales=x_scales[g][:, cols], in_=x_grouped[:]
+                out=x_codes[g][:, cols].bitcast(FP8X4),
+                scales=x_scales[g][:, cols],
+                in_=x_grouped[g, q][:],
             )
 
         def node_major_bank(g, l):
@@ -126,17 +151,16 @@ def tile_avwgcn_pb_t_kernel(tc, x, adj, out_0, out_1):
                     start=True,
                     stop=True,
                 )
-            x1_grouped = hop_pool.tile([P, P, PACK], BF16, align_bytes=64)
+            x1_grouped[l] = hop_pool.tile([P, P, PACK], BF16, align_bytes=64, name="x1_grouped")
             copy_out = nc.vector.tensor_copy if l % 4 == 3 else nc.scalar.copy
-            copy_out(out=x1_grouped[:], in_=bank[:].rearrange("p t s -> p s t"))
-            return x1_grouped
+            copy_out(out=x1_grouped[l][:], in_=bank[:].rearrange("p t s -> p s t"))
 
-        def quantise_x1(g, l, x1_grouped):
+        def quantise_x1(g, l):
             cols = slice(l * P, (l + 1) * P)
             nc.vector.quantize_mx(
                 out=x1_codes[g][:, cols].bitcast(FP8X4),
                 scales=x1_scales[g][:, cols],
-                in_=x1_grouped[:].rearrange("p s t -> p (s t)"),
+                in_=x1_grouped[l][:].rearrange("p s t -> p (s t)"),
             )
 
         def series_major_bank(result, hop, codes, scales, n, q):
@@ -162,31 +186,42 @@ def tile_avwgcn_pb_t_kernel(tc, x, adj, out_0, out_1):
                 in_=result[:].rearrange("p w l -> p (w l)"),
             )
 
-        for q in range(QUADS):
-            quantise_x(0, q)
+        for stage in range(QUADS + 2):
+            if stage < QUADS:
+                sort_x(0, stage)
+            if 1 <= stage <= QUADS:
+                transpose_x(0, stage - 1)
+            if stage >= 2:
+                quantise_x(0, stage - 2)
+
         for g in range(BLOCKS + 1):
             first_hop = g < BLOCKS
             second_hop = g >= 1
+            next_block = g + 1 < BLOCKS
             if first_hop:
                 new_operand(x1_codes, x1_scales, g, "x1")
             for n in range(NODE_TILES):
-                x1_grouped = {}
+                if next_block and n < QUADS:
+                    sort_x(g + 1, n)
+                if next_block and n >= 1:
+                    quantise_x(g + 1, n - 1)
                 if first_hop:
                     result_1 = out_pool.tile([P, P, STEPS], F32, tag="result")
                 if second_hop:
                     result_2 = out_pool.tile([P, P, STEPS], F32, tag="result")
                 for q in range(QUADS):
+                    l = n * QUADS + q
                     if first_hop:
-                        l = n * QUADS + q
-                        x1_grouped[l] = node_major_bank(g, l)
+                        node_major_bank(g, l)
                         series_major_bank(result_1, 0, x_codes[g], x_scales[g], n, q)
                     if second_hop:
                         series_major_bank(result_2, 1, x1_codes[g - 1], x1_scales[g - 1], n, q)
+                    if first_hop and q >= 1:
+                        quantise_x1(g, l - 1)
                 if first_hop:
+                    quantise_x1(g, n * QUADS + QUADS - 1)
                     store(0, g, n, result_1)
                 if second_hop:
                     store(1, g - 1, n, result_2)
-                for l in x1_grouped:
-                    quantise_x1(g, l, x1_grouped[l])
-                if g + 1 < BLOCKS and n < QUADS:
-                    quantise_x(g + 1, n)
+                if next_block and n < QUADS:
+                    transpose_x(g + 1, n)

@@ -32,15 +32,12 @@ def tile_avwgcn_pb_t_kernel(tc, x, adj, out_0, out_1):
 
     with ExitStack() as ctx:
         keep = ctx.enter_context(tc.tile_pool(name="keep", bufs=1))
-        sort_pool = ctx.enter_context(tc.tile_pool(name="sort", bufs=4))
-        group_pool = ctx.enter_context(tc.tile_pool(name="group", bufs=3))
-        hop_pool = ctx.enter_context(tc.tile_pool(name="hop", bufs=6))
+        sort_pool = ctx.enter_context(tc.tile_pool(name="sort", bufs=6))
+        group_pool = ctx.enter_context(tc.tile_pool(name="group", bufs=4))
+        hop_pool = ctx.enter_context(tc.tile_pool(name="hop", bufs=2))
         code_pool = ctx.enter_context(tc.tile_pool(name="codes", bufs=2))
         out_pool = ctx.enter_context(tc.tile_pool(name="outs", bufs=12))
-        psum_t = ctx.enter_context(tc.psum_pool(name="psum_t", bufs=2))
-        psum_n = ctx.enter_context(tc.psum_pool(name="psum_n", bufs=2))
-        psum_s = ctx.enter_context(tc.psum_pool(name="psum_s", bufs=4))
-        ctx.enter_context(tc.manual_schedule())
+        psum = ctx.enter_context(tc.psum_pool(name="psum", bufs=8))
 
         adj_raw = keep.tile([P, PACK, NODES], BF16)
         nc.sync.dma_start(out=adj_raw[:], in_=adj.rearrange("(p j) w -> p j w", j=PACK))
@@ -78,69 +75,45 @@ def tile_avwgcn_pb_t_kernel(tc, x, adj, out_0, out_1):
         x_scales = {}
         x1_codes = {}
         x1_scales = {}
-        x_sorted = {}
-        x_grouped = {}
-        x1_grouped = {}
 
         def new_operand(codes, scales, g, name):
             codes[g] = code_pool.tile([P, STEPS * P], U32, align_bytes=64, name=name + "_codes")
             scales[g] = code_pool.tile([P, STEPS * P], U8, align_bytes=64, name=name + "_scales")
 
-        def sort_x(g, q):
-            x_sorted[g, q] = sort_pool.tile([P, 4 * NODES], BF16, name="x_sorted")
+        def quantise_x(g, q):
+            if q == 0:
+                new_operand(x_codes, x_scales, g, "x")
+            x_sorted = sort_pool.tile([P, 4 * NODES], BF16)
             src = x_in[g][:].rearrange("p (i u e l) -> p u i e l", u=2, e=2, l=STEPS)
-            dst = x_sorted[g, q][:].rearrange("p (l u i e) -> p u i e l", l=4, u=2, e=2)
+            dst = x_sorted[:].rearrange("p (l u i e) -> p u i e l", l=4, u=2, e=2)
             for u in range(2):
-                if g == 0:
-                    nc.vector.tensor_copy(out=dst[:, u], in_=src[:, u, :, :, 4 * q : 4 * q + 4])
-                else:
-                    nc.gpsimd.tensor_scalar(
-                        out=dst[:, u],
-                        in0=src[:, u, :, :, 4 * q : 4 * q + 4],
-                        scalar1=1.0,
-                        scalar2=0.0,
-                        op0=mybir.AluOpType.mult,
-                        op1=mybir.AluOpType.add,
-                    )
+                nc.vector.tensor_copy(out=dst[:, u], in_=src[:, u, :, :, 4 * q : 4 * q + 4])
+            words = x_sorted[:].bitcast(F32)
 
-        def transpose_x(g, q):
-            words = x_sorted[g, q][:].bitcast(F32)
-            x_grouped[g, q] = group_pool.tile(
-                [P, 4 * P * PACK], BF16, align_bytes=64, name="x_grouped"
-            )
-            grouped_words = x_grouped[g, q][:].bitcast(F32)
-            banks = []
+            x_grouped = group_pool.tile([P, 4 * P * PACK], BF16, align_bytes=64)
+            grouped_words = x_grouped[:].bitcast(F32)
             for h in range(2):
-                bank = psum_t.tile([P, BANK], F32, name="bank_t")
+                bank = psum.tile([P, BANK], F32, name="bank_t", tag="bank")
                 for c in range(4):
                     nc.tensor.transpose(
                         bank[:, c * P : (c + 1) * P],
                         words[:, (4 * h + c) * P : (4 * h + c + 1) * P],
                         ident[:],
                     )
-                banks.append(bank)
-            for h in range(2):
-                copy_out = nc.vector.tensor_copy if h == 0 else nc.scalar.copy
-                copy_out(
+                nc.scalar.copy(
                     out=grouped_words[:, h * BANK : (h + 1) * BANK].rearrange(
                         "p (l s u) -> p l s u", l=2, u=2
                     ),
-                    in_=banks[h][:].rearrange("p (l u s) -> p l s u", l=2, u=2),
+                    in_=bank[:].rearrange("p (l u s) -> p l s u", l=2, u=2),
                 )
-
-        def quantise_x(g, q):
-            if q == 0:
-                new_operand(x_codes, x_scales, g, "x")
             cols = slice(q * 4 * P, (q + 1) * 4 * P)
             nc.vector.quantize_mx(
-                out=x_codes[g][:, cols].bitcast(FP8X4),
-                scales=x_scales[g][:, cols],
-                in_=x_grouped[g, q][:],
+                out=x_codes[g][:, cols].bitcast(FP8X4), scales=x_scales[g][:, cols], in_=x_grouped[:]
             )
 
         def node_major_bank(g, l):
             cols = slice(l * P, (l + 1) * P)
-            bank = psum_n.tile([P, PACK, P], F32, name="bank_n")
+            bank = psum.tile([P, PACK, P], F32, name="bank_n", tag="bank")
             for t in range(PACK):
                 nc.tensor.matmul_mx(
                     out=bank[:, t, :],
@@ -151,21 +124,21 @@ def tile_avwgcn_pb_t_kernel(tc, x, adj, out_0, out_1):
                     start=True,
                     stop=True,
                 )
-            x1_grouped[l] = hop_pool.tile([P, P, PACK], BF16, align_bytes=64, name="x1_grouped")
-            copy_out = nc.vector.tensor_copy if l % 4 == 3 else nc.scalar.copy
-            copy_out(out=x1_grouped[l][:], in_=bank[:].rearrange("p t s -> p s t"))
-
-        def quantise_x1(g, l):
-            cols = slice(l * P, (l + 1) * P)
-            nc.vector.quantize_mx(
-                out=x1_codes[g][:, cols].bitcast(FP8X4),
-                scales=x1_scales[g][:, cols],
-                in_=x1_grouped[l][:].rearrange("p s t -> p (s t)"),
-            )
+            if l % 4 == 0:
+                x1_grouped[g] = hop_pool.tile([P, 4, P, PACK], BF16, align_bytes=64, name="x1_grouped")
+            copy_out = nc.vector.tensor_copy if l % 4 == 0 else nc.scalar.copy
+            copy_out(out=x1_grouped[g][:, l % 4], in_=bank[:].rearrange("p t s -> p s t"))
+            if l % 4 == 3:
+                quad_cols = slice((l - 3) * P, (l + 1) * P)
+                nc.vector.quantize_mx(
+                    out=x1_codes[g][:, quad_cols].bitcast(FP8X4),
+                    scales=x1_scales[g][:, quad_cols],
+                    in_=x1_grouped[g][:].rearrange("p l s t -> p (l s t)"),
+                )
 
         def series_major_bank(result, hop, codes, scales, n, q):
             node_cols = slice(n * P, (n + 1) * P)
-            bank = psum_s.tile([P, 4, P], F32, name="bank_s")
+            bank = psum.tile([P, 4, P], F32, name="bank_s", tag="bank")
             for j in range(4):
                 cols = slice((4 * q + j) * P, (4 * q + j + 1) * P)
                 nc.tensor.matmul_mx(
@@ -186,42 +159,44 @@ def tile_avwgcn_pb_t_kernel(tc, x, adj, out_0, out_1):
                 in_=result[:].rearrange("p w l -> p (w l)"),
             )
 
-        for stage in range(QUADS + 2):
-            if stage < QUADS:
-                sort_x(0, stage)
-            if 1 <= stage <= QUADS:
-                transpose_x(0, stage - 1)
-            if stage >= 2:
-                quantise_x(0, stage - 2)
-
+        x1_grouped = {}
+        half_tiles = NODE_TILES // 2
+        for q in range(QUADS):
+            quantise_x(0, q)
         for g in range(BLOCKS + 1):
-            first_hop = g < BLOCKS
-            second_hop = g >= 1
+            this_block = g < BLOCKS
+            last_block = g >= 1
             next_block = g + 1 < BLOCKS
-            if first_hop:
+            if this_block:
                 new_operand(x1_codes, x1_scales, g, "x1")
-            for n in range(NODE_TILES):
-                if next_block and n < QUADS:
-                    sort_x(g + 1, n)
-                if next_block and n >= 1:
-                    quantise_x(g + 1, n - 1)
-                if first_hop:
+            for j in range(half_tiles):
+                if this_block:
                     result_1 = out_pool.tile([P, P, STEPS], F32, tag="result")
-                if second_hop:
+                if last_block:
                     result_2 = out_pool.tile([P, P, STEPS], F32, tag="result")
                 for q in range(QUADS):
-                    l = n * QUADS + q
-                    if first_hop:
+                    if this_block:
+                        l = 2 * (j * QUADS + q)
                         node_major_bank(g, l)
-                        series_major_bank(result_1, 0, x_codes[g], x_scales[g], n, q)
-                    if second_hop:
-                        series_major_bank(result_2, 1, x1_codes[g - 1], x1_scales[g - 1], n, q)
-                    if first_hop and q >= 1:
-                        quantise_x1(g, l - 1)
-                if first_hop:
-                    quantise_x1(g, n * QUADS + QUADS - 1)
-                    store(0, g, n, result_1)
-                if second_hop:
-                    store(1, g - 1, n, result_2)
-                if next_block and n < QUADS:
-                    transpose_x(g + 1, n)
+                        node_major_bank(g, l + 1)
+                        series_major_bank(result_1, 0, x_codes[g], x_scales[g], j, q)
+                    if last_block:
+                        series_major_bank(
+                            result_2, 1, x1_codes[g - 1], x1_scales[g - 1], half_tiles + j, q
+                        )
+                if this_block:
+                    store(0, g, j, result_1)
+                if last_block:
+                    store(1, g - 1, half_tiles + j, result_2)
+            if this_block:
+                for j in range(half_tiles):
+                    result_1 = out_pool.tile([P, P, STEPS], F32, tag="result")
+                    result_2 = out_pool.tile([P, P, STEPS], F32, tag="result")
+                    for q in range(QUADS):
+                        turn = j * QUADS + q
+                        if next_block and turn % 2 == 0:
+                            quantise_x(g + 1, turn // 2)
+                        series_major_bank(result_1, 0, x_codes[g], x_scales[g], half_tiles + j, q)
+                        series_major_bank(result_2, 1, x1_codes[g], x1_scales[g], j, q)
+                    store(0, g, half_tiles + j, result_1)
+                    store(1, g, j, result_2)

@@ -15,9 +15,11 @@ NODES = P * PACK
 STEPS = 12
 SERIES = 8 * 64
 BLOCKS = SERIES // P
-QUADS = STEPS // 4
-NODE_TILES = NODES // P
 BANK = 512
+QUAD = BANK // P
+QUADS = STEPS // QUAD
+NODE_TILES = NODES // P
+TURNS = (NODE_TILES // 2) * QUADS
 
 FLOPS = 2 * 2 * SERIES * STEPS * NODES * NODES
 
@@ -75,6 +77,7 @@ def tile_avwgcn_pb_t_kernel(tc, x, adj, out_0, out_1):
         x_scales = {}
         x1_codes = {}
         x1_scales = {}
+        x1_grouped = {}
 
         def new_operand(codes, scales, g, name):
             codes[g] = code_pool.tile([P, STEPS * P], U32, align_bytes=64, name=name + "_codes")
@@ -83,14 +86,16 @@ def tile_avwgcn_pb_t_kernel(tc, x, adj, out_0, out_1):
         def quantise_x(g, q):
             if q == 0:
                 new_operand(x_codes, x_scales, g, "x")
-            x_sorted = sort_pool.tile([P, 4 * NODES], BF16)
+            x_sorted = sort_pool.tile([P, QUAD * NODES], BF16)
             src = x_in[g][:].rearrange("p (i u e l) -> p u i e l", u=2, e=2, l=STEPS)
-            dst = x_sorted[:].rearrange("p (l u i e) -> p u i e l", l=4, u=2, e=2)
+            dst = x_sorted[:].rearrange("p (l u i e) -> p u i e l", l=QUAD, u=2, e=2)
             for u in range(2):
-                nc.vector.tensor_copy(out=dst[:, u], in_=src[:, u, :, :, 4 * q : 4 * q + 4])
+                nc.vector.tensor_copy(
+                    out=dst[:, u], in_=src[:, u, :, :, QUAD * q : QUAD * (q + 1)]
+                )
             words = x_sorted[:].bitcast(F32)
 
-            x_grouped = group_pool.tile([P, 4 * P * PACK], BF16, align_bytes=64)
+            x_grouped = group_pool.tile([P, QUAD * P * PACK], BF16, align_bytes=64)
             grouped_words = x_grouped[:].bitcast(F32)
             for h in range(2):
                 bank = psum.tile([P, BANK], F32, name="bank_t", tag="bank")
@@ -106,7 +111,7 @@ def tile_avwgcn_pb_t_kernel(tc, x, adj, out_0, out_1):
                     ),
                     in_=bank[:].rearrange("p (l u s) -> p l s u", l=2, u=2),
                 )
-            cols = slice(q * 4 * P, (q + 1) * 4 * P)
+            cols = slice(q * QUAD * P, (q + 1) * QUAD * P)
             nc.vector.quantize_mx(
                 out=x_codes[g][:, cols].bitcast(FP8X4), scales=x_scales[g][:, cols], in_=x_grouped[:]
             )
@@ -124,25 +129,27 @@ def tile_avwgcn_pb_t_kernel(tc, x, adj, out_0, out_1):
                     start=True,
                     stop=True,
                 )
-            if l % 4 == 0:
-                x1_grouped[g] = hop_pool.tile([P, 4, P, PACK], BF16, align_bytes=64, name="x1_grouped")
-            copy_out = nc.vector.tensor_copy if l % 4 == 0 else nc.scalar.copy
-            copy_out(out=x1_grouped[g][:, l % 4], in_=bank[:].rearrange("p t s -> p s t"))
-            if l % 4 == 3:
-                quad_cols = slice((l - 3) * P, (l + 1) * P)
+            if l % QUAD == 0:
+                x1_grouped[g] = hop_pool.tile(
+                    [P, QUAD, P, PACK], BF16, align_bytes=64, name="x1_grouped"
+                )
+            copy_out = nc.vector.tensor_copy if l % QUAD == 0 else nc.scalar.copy
+            copy_out(out=x1_grouped[g][:, l % QUAD], in_=bank[:].rearrange("p t s -> p s t"))
+            if l % QUAD == QUAD - 1:
+                quad_cols = slice((l + 1 - QUAD) * P, (l + 1) * P)
                 nc.vector.quantize_mx(
                     out=x1_codes[g][:, quad_cols].bitcast(FP8X4),
                     scales=x1_scales[g][:, quad_cols],
                     in_=x1_grouped[g][:].rearrange("p l s t -> p (l s t)"),
                 )
 
-        def series_major_bank(result, hop, codes, scales, n, q):
+        def series_major_bank(result, codes, scales, n, q):
             node_cols = slice(n * P, (n + 1) * P)
-            bank = psum.tile([P, 4, P], F32, name="bank_s", tag="bank")
-            for j in range(4):
-                cols = slice((4 * q + j) * P, (4 * q + j + 1) * P)
+            bank = psum.tile([P, QUAD, P], F32, name="bank_s", tag="bank")
+            for k in range(QUAD):
+                cols = slice((QUAD * q + k) * P, (QUAD * q + k + 1) * P)
                 nc.tensor.matmul_mx(
-                    out=bank[:, j, :],
+                    out=bank[:, k, :],
                     lhsT=codes[:, cols].bitcast(FP8X4),
                     lhsT_scale=scales[:, cols],
                     rhs=adj_nat_codes[:, node_cols].bitcast(FP8X4),
@@ -150,8 +157,10 @@ def tile_avwgcn_pb_t_kernel(tc, x, adj, out_0, out_1):
                     start=True,
                     stop=True,
                 )
-            copy_out = nc.scalar.copy if (hop + n) % 2 == 0 else nc.vector.tensor_copy
-            copy_out(out=result[:, :, 4 * q : 4 * q + 4], in_=bank[:].rearrange("p l w -> p w l"))
+            copy_out = nc.scalar.copy if n % 2 == 0 else nc.vector.tensor_copy
+            copy_out(
+                out=result[:, :, QUAD * q : QUAD * (q + 1)], in_=bank[:].rearrange("p l w -> p w l")
+            )
 
         def store(hop, g, n, result):
             nc.sync.dma_start(
@@ -159,44 +168,29 @@ def tile_avwgcn_pb_t_kernel(tc, x, adj, out_0, out_1):
                 in_=result[:].rearrange("p w l -> p (w l)"),
             )
 
-        x1_grouped = {}
-        half_tiles = NODE_TILES // 2
         for q in range(QUADS):
             quantise_x(0, q)
-        for g in range(BLOCKS + 1):
-            this_block = g < BLOCKS
-            last_block = g >= 1
-            next_block = g + 1 < BLOCKS
-            if this_block:
-                new_operand(x1_codes, x1_scales, g, "x1")
-            for j in range(half_tiles):
-                if this_block:
-                    result_1 = out_pool.tile([P, P, STEPS], F32, tag="result")
-                if last_block:
-                    result_2 = out_pool.tile([P, P, STEPS], F32, tag="result")
+        for g in range(BLOCKS):
+            new_operand(x1_codes, x1_scales, g, "x1")
+            for pair in range(NODE_TILES // 2):
+                result_even = out_pool.tile([P, P, STEPS], F32, tag="result")
+                result_odd = out_pool.tile([P, P, STEPS], F32, tag="result")
                 for q in range(QUADS):
-                    if this_block:
-                        l = 2 * (j * QUADS + q)
+                    turn = pair * QUADS + q
+                    for l in range(turn * STEPS // TURNS, (turn + 1) * STEPS // TURNS):
                         node_major_bank(g, l)
-                        node_major_bank(g, l + 1)
-                        series_major_bank(result_1, 0, x_codes[g], x_scales[g], j, q)
-                    if last_block:
-                        series_major_bank(
-                            result_2, 1, x1_codes[g - 1], x1_scales[g - 1], half_tiles + j, q
-                        )
-                if this_block:
-                    store(0, g, j, result_1)
-                if last_block:
-                    store(1, g - 1, half_tiles + j, result_2)
-            if this_block:
-                for j in range(half_tiles):
-                    result_1 = out_pool.tile([P, P, STEPS], F32, tag="result")
-                    result_2 = out_pool.tile([P, P, STEPS], F32, tag="result")
-                    for q in range(QUADS):
-                        turn = j * QUADS + q
-                        if next_block and turn % 2 == 0:
-                            quantise_x(g + 1, turn // 2)
-                        series_major_bank(result_1, 0, x_codes[g], x_scales[g], half_tiles + j, q)
-                        series_major_bank(result_2, 1, x1_codes[g], x1_scales[g], j, q)
-                    store(0, g, half_tiles + j, result_1)
-                    store(1, g, j, result_2)
+                    series_major_bank(result_even, x_codes[g], x_scales[g], 2 * pair, q)
+                    series_major_bank(result_odd, x_codes[g], x_scales[g], 2 * pair + 1, q)
+                store(0, g, 2 * pair, result_even)
+                store(0, g, 2 * pair + 1, result_odd)
+            for pair in range(NODE_TILES // 2):
+                result_even = out_pool.tile([P, P, STEPS], F32, tag="result")
+                result_odd = out_pool.tile([P, P, STEPS], F32, tag="result")
+                for q in range(QUADS):
+                    turn = pair * QUADS + q
+                    if g + 1 < BLOCKS and turn % 2 == 0:
+                        quantise_x(g + 1, turn // 2)
+                    series_major_bank(result_even, x1_codes[g], x1_scales[g], 2 * pair, q)
+                    series_major_bank(result_odd, x1_codes[g], x1_scales[g], 2 * pair + 1, q)
+                store(1, g, 2 * pair, result_even)
+                store(1, g, 2 * pair + 1, result_odd)

@@ -89,10 +89,24 @@ def tile_avwgcn_pb_t_kernel(tc, x, adj, out_0, out_1):
             x_sorted = sort_pool.tile([P, QUAD * NODES], BF16)
             src = x_in[g][:].rearrange("p (i u e l) -> p u i e l", u=2, e=2, l=STEPS)
             dst = x_sorted[:].rearrange("p (l u i e) -> p u i e l", l=QUAD, u=2, e=2)
-            for u in range(2):
-                nc.vector.tensor_copy(
-                    out=dst[:, u], in_=src[:, u, :, :, QUAD * q : QUAD * (q + 1)]
-                )
+            if g == 0:
+                for u in range(2):
+                    nc.vector.tensor_copy(
+                        out=dst[:, u], in_=src[:, u, :, :, QUAD * q : QUAD * (q + 1)]
+                    )
+            else:
+                src_l = x_in[g][:].rearrange("p (i u e l) -> p u l i e", u=2, e=2, l=STEPS)
+                dst_l = x_sorted[:].rearrange("p (l u i e) -> p u l i e", l=QUAD, u=2, e=2)
+                for u in range(2):
+                    for h in range(2):
+                        nc.gpsimd.tensor_scalar(
+                            out=dst_l[:, u, 2 * h : 2 * h + 2],
+                            in0=src_l[:, u, QUAD * q + 2 * h : QUAD * q + 2 * h + 2],
+                            scalar1=1.0,
+                            scalar2=0.0,
+                            op0=mybir.AluOpType.mult,
+                            op1=mybir.AluOpType.add,
+                        )
             words = x_sorted[:].bitcast(F32)
 
             x_grouped = group_pool.tile([P, QUAD * P * PACK], BF16, align_bytes=64)
@@ -133,7 +147,8 @@ def tile_avwgcn_pb_t_kernel(tc, x, adj, out_0, out_1):
                 x1_grouped[g] = hop_pool.tile(
                     [P, QUAD, P, PACK], BF16, align_bytes=64, name="x1_grouped"
                 )
-            copy_out = nc.vector.tensor_copy if l % QUAD == 0 else nc.scalar.copy
+            on_vector = l % QUAD == 0 or (l % QUAD == 2 and l < 2 * QUAD)
+            copy_out = nc.vector.tensor_copy if on_vector else nc.scalar.copy
             copy_out(out=x1_grouped[g][:, l % QUAD], in_=bank[:].rearrange("p t s -> p s t"))
             if l % QUAD == QUAD - 1:
                 quad_cols = slice((l + 1 - QUAD) * P, (l + 1) * P)

@@ -95,13 +95,11 @@ def tile_avwgcn_pb_t_kernel(tc, x, adj, out_0, out_1):
                         out=dst[:, u], in_=src[:, u, :, :, QUAD * q : QUAD * (q + 1)]
                     )
             else:
-                src_l = x_in[g][:].rearrange("p (i u e l) -> p u l i e", u=2, e=2, l=STEPS)
-                dst_l = x_sorted[:].rearrange("p (l u i e) -> p u l i e", l=QUAD, u=2, e=2)
                 for u in range(2):
                     for h in range(2):
                         nc.gpsimd.tensor_scalar(
-                            out=dst_l[:, u, 2 * h : 2 * h + 2],
-                            in0=src_l[:, u, QUAD * q + 2 * h : QUAD * q + 2 * h + 2],
+                            out=dst[:, u, 64 * h : 64 * h + 64],
+                            in0=src[:, u, 64 * h : 64 * h + 64, :, QUAD * q : QUAD * (q + 1)],
                             scalar1=1.0,
                             scalar2=0.0,
                             op0=mybir.AluOpType.mult,

@@ -87,19 +87,19 @@ def tile_avwgcn_pb_t_kernel(tc, x, adj, out_0, out_1):
             if q == 0:
                 new_operand(x_codes, x_scales, g, "x")
             x_sorted = sort_pool.tile([P, QUAD * NODES], BF16)
-            src = x_in[g][:].rearrange("p (i u e l) -> p u i e l", u=2, e=2, l=STEPS)
-            dst = x_sorted[:].rearrange("p (l u i e) -> p u i e l", l=QUAD, u=2, e=2)
+            src = x_in[g][:].rearrange("p (i u e l) -> p u i l e", u=2, e=2, l=STEPS)
+            dst = x_sorted[:].rearrange("p (u i l e) -> p u i l e", u=2, l=QUAD, e=2)
             if g == 0:
                 for u in range(2):
                     nc.vector.tensor_copy(
-                        out=dst[:, u], in_=src[:, u, :, :, QUAD * q : QUAD * (q + 1)]
+                        out=dst[:, u], in_=src[:, u, :, QUAD * q : QUAD * (q + 1), :]
                     )
             else:
                 for u in range(2):
                     for h in range(2):
                         nc.gpsimd.tensor_scalar(
                             out=dst[:, u, 64 * h : 64 * h + 64],
-                            in0=src[:, u, 64 * h : 64 * h + 64, :, QUAD * q : QUAD * (q + 1)],
+                            in0=src[:, u, 64 * h : 64 * h + 64, QUAD * q : QUAD * (q + 1), :],
                             scalar1=1.0,
                             scalar2=0.0,
                             op0=mybir.AluOpType.mult,
@@ -112,9 +112,10 @@ def tile_avwgcn_pb_t_kernel(tc, x, adj, out_0, out_1):
             for h in range(2):
                 bank = psum.tile([P, BANK], F32, name="bank_t", tag="bank")
                 for c in range(4):
+                    first = (c % 2) * QUAD * P + 2 * h + c // 2
                     nc.tensor.transpose(
                         bank[:, c * P : (c + 1) * P],
-                        words[:, (4 * h + c) * P : (4 * h + c + 1) * P],
+                        words[:, first : first + QUAD * (P - 1) + 1 : QUAD],
                         ident[:],
                     )
                 nc.scalar.copy(

@@ -88,7 +88,7 @@ def tile_avwgcn_pb_t_kernel(tc, x, adj, out_0, out_1):
                 new_operand(x_codes, x_scales, g, "x")
             x_sorted = sort_pool.tile([P, QUAD * NODES], BF16)
             src = x_in[g][:].rearrange("p (i u e l) -> p u i l e", u=2, e=2, l=STEPS)
-            dst = x_sorted[:].rearrange("p (u i l e) -> p u i l e", u=2, l=QUAD, e=2)
+            dst = x_sorted[:].rearrange("p (l u i e) -> p u i l e", l=QUAD, u=2, e=2)
             if g == 0:
                 for u in range(2):
                     nc.vector.tensor_copy(
@@ -112,10 +112,9 @@ def tile_avwgcn_pb_t_kernel(tc, x, adj, out_0, out_1):
             for h in range(2):
                 bank = psum.tile([P, BANK], F32, name="bank_t", tag="bank")
                 for c in range(4):
-                    first = (c % 2) * QUAD * P + 2 * h + c // 2
                     nc.tensor.transpose(
                         bank[:, c * P : (c + 1) * P],
-                        words[:, first : first + QUAD * (P - 1) + 1 : QUAD],
+                        words[:, (4 * h + c) * P : (4 * h + c + 1) * P],
                         ident[:],
                     )
                 nc.scalar.copy(

from contextlib import ExitStack

import concourse.mybir as mybir
from concourse.masks import make_identity

BF16 = mybir.dt.bfloat16
F32 = mybir.dt.float32
U32 = mybir.dt.uint32
U8 = mybir.dt.uint8
FP8X4 = mybir.dt.float8_e4m3fn_x4

P = 128
PACK = 4
NODES = P * PACK
STEPS = 12
SERIES = 8 * 64
BLOCKS = SERIES // P
BANK = 512
QUAD = BANK // P
QUADS = STEPS // QUAD
NODE_TILES = NODES // P
TURNS = (NODE_TILES // 2) * QUADS

FLOPS = 2 * 2 * SERIES * STEPS * NODES * NODES


def tile_avwgcn_pb_t_kernel(tc, x, adj, out_0, out_1):
    nc = tc.nc
    x_rows = x.rearrange("b c v l -> (b c) (v l)")
    out_rows = [
        out_0.rearrange("b c w l -> (b c) (w l)"),
        out_1.rearrange("b c w l -> (b c) (w l)"),
    ]

    with ExitStack() as ctx:
        keep = ctx.enter_context(tc.tile_pool(name="keep", bufs=1))
        sort_pool = ctx.enter_context(tc.tile_pool(name="sort", bufs=6))
        group_pool = ctx.enter_context(tc.tile_pool(name="group", bufs=4))
        hop_pool = ctx.enter_context(tc.tile_pool(name="hop", bufs=2))
        code_pool = ctx.enter_context(tc.tile_pool(name="codes", bufs=2))
        out_pool = ctx.enter_context(tc.tile_pool(name="outs", bufs=12))
        psum = ctx.enter_context(tc.psum_pool(name="psum", bufs=8))

        adj_raw = keep.tile([P, PACK, NODES], BF16)
        nc.sync.dma_start(out=adj_raw[:], in_=adj.rearrange("(p j) w -> p j w", j=PACK))
        x_in = []
        for g in range(BLOCKS):
            x_block = keep.tile([P, NODES * STEPS], BF16, name="x_in%d" % g)
            nc.sync.dma_start(out=x_block[:], in_=x_rows[g * P : (g + 1) * P, :])
            x_in.append(x_block)

        ident = keep.tile([P, P], F32)
        make_identity(nc, ident[:])

        adj_nat_grouped = keep.tile([P, NODES, PACK], BF16, align_bytes=64)
        nc.vector.tensor_copy(out=adj_nat_grouped[:], in_=adj_raw[:].rearrange("p j w -> p w j"))
        adj_mod_grouped = keep.tile([P, PACK, P, PACK], BF16, align_bytes=64)
        nc.scalar.copy(
            out=adj_mod_grouped[:], in_=adj_raw[:].rearrange("p j (m t) -> p t m j", t=PACK)
        )
        adj_nat_codes = keep.tile([P, NODES], U32, align_bytes=64)
        adj_nat_scales = keep.tile([P, NODES], U8, align_bytes=64)
        nc.vector.quantize_mx(
            out=adj_nat_codes[:].bitcast(FP8X4),
            scales=adj_nat_scales[:],
            in_=adj_nat_grouped[:].rearrange("p w j -> p (w j)"),
        )
        adj_mod_codes = keep.tile([P, NODES], U32, align_bytes=64)
        adj_mod_scales = keep.tile([P, NODES], U8, align_bytes=64)
        nc.vector.quantize_mx(
            out=adj_mod_codes[:].bitcast(FP8X4),
            scales=adj_mod_scales[:],
            in_=adj_mod_grouped[:].rearrange("p t m j -> p (t m j)"),
        )

        x_codes = {}
        x_scales = {}
        x1_codes = {}
        x1_scales = {}
        x1_grouped = {}

        def new_operand(codes, scales, g, name):
            codes[g] = code_pool.tile([P, STEPS * P], U32, align_bytes=64, name=name + "_codes")
            scales[g] = code_pool.tile([P, STEPS * P], U8, align_bytes=64, name=name + "_scales")

        def quantise_x(g, q):
            if q == 0:
                new_operand(x_codes, x_scales, g, "x")
            x_sorted = sort_pool.tile([P, QUAD * NODES], BF16)
            src = x_in[g][:].rearrange("p (i u e l) -> p u i l e", u=2, e=2, l=STEPS)
            dst = x_sorted[:].rearrange("p (l u i e) -> p u i l e", l=QUAD, u=2, e=2)
            if g == 0:
                for u in range(2):
                    nc.vector.tensor_copy(
                        out=dst[:, u], in_=src[:, u, :, QUAD * q : QUAD * (q + 1), :]
                    )
            else:
                for u in range(2):
                    for h in range(2):
                        nc.gpsimd.tensor_scalar(
                            out=dst[:, u, 64 * h : 64 * h + 64],
                            in0=src[:, u, 64 * h : 64 * h + 64, QUAD * q : QUAD * (q + 1), :],
                            scalar1=1.0,
                            scalar2=0.0,
                            op0=mybir.AluOpType.mult,
                            op1=mybir.AluOpType.add,
                        )
            words = x_sorted[:].bitcast(F32)

            x_grouped = group_pool.tile([P, QUAD * P * PACK], BF16, align_bytes=64)
            grouped_words = x_grouped[:].bitcast(F32)
            for h in range(2):
                bank = psum.tile([P, BANK], F32, name="bank_t", tag="bank")
                for c in range(4):
                    nc.tensor.transpose(
                        bank[:, c * P : (c + 1) * P],
                        words[:, (4 * h + c) * P : (4 * h + c + 1) * P],
                        ident[:],
                    )
                nc.scalar.copy(
                    out=grouped_words[:, h * BANK : (h + 1) * BANK].rearrange(
                        "p (l s u) -> p l s u", l=2, u=2
                    ),
                    in_=bank[:].rearrange("p (l u s) -> p l s u", l=2, u=2),
                )
            cols = slice(q * QUAD * P, (q + 1) * QUAD * P)
            nc.vector.quantize_mx(
                out=x_codes[g][:, cols].bitcast(FP8X4), scales=x_scales[g][:, cols], in_=x_grouped[:]
            )

        def node_major_bank(g, l):
            cols = slice(l * P, (l + 1) * P)
            bank = psum.tile([P, PACK, P], F32, name="bank_n", tag="bank")
            for t in range(PACK):
                nc.tensor.matmul_mx(
                    out=bank[:, t, :],
                    lhsT=adj_mod_codes[:, t * P : (t + 1) * P].bitcast(FP8X4),
                    lhsT_scale=adj_mod_scales[:, t * P : (t + 1) * P],
                    rhs=x_codes[g][:, cols].bitcast(FP8X4),
                    rhs_scale=x_scales[g][:, cols],
                    start=True,
                    stop=True,
                )
            if l % QUAD == 0:
                x1_grouped[g] = hop_pool.tile(
                    [P, QUAD, P, PACK], BF16, align_bytes=64, name="x1_grouped"
                )
            on_vector = l % QUAD == 0 or (l % QUAD == 2 and l < 2 * QUAD)
            copy_out = nc.vector.tensor_copy if on_vector else nc.scalar.copy
            copy_out(out=x1_grouped[g][:, l % QUAD], in_=bank[:].rearrange("p t s -> p s t"))
            if l % QUAD == QUAD - 1:
                quad_cols = slice((l + 1 - QUAD) * P, (l + 1) * P)
                nc.vector.quantize_mx(
                    out=x1_codes[g][:, quad_cols].bitcast(FP8X4),
                    scales=x1_scales[g][:, quad_cols],
                    in_=x1_grouped[g][:].rearrange("p l s t -> p (l s t)"),
                )

        def series_major_bank(result, codes, scales, n, q):
            node_cols = slice(n * P, (n + 1) * P)
            bank = psum.tile([P, QUAD, P], F32, name="bank_s", tag="bank")
            for k in range(QUAD):
                cols = slice((QUAD * q + k) * P, (QUAD * q + k + 1) * P)
                nc.tensor.matmul_mx(
                    out=bank[:, k, :],
                    lhsT=codes[:, cols].bitcast(FP8X4),
                    lhsT_scale=scales[:, cols],
                    rhs=adj_nat_codes[:, node_cols].bitcast(FP8X4),
                    rhs_scale=adj_nat_scales[:, node_cols],
                    start=True,
                    stop=True,
                )
            copy_out = nc.scalar.copy if n % 2 == 0 else nc.vector.tensor_copy
            copy_out(
                out=result[:, :, QUAD * q : QUAD * (q + 1)], in_=bank[:].rearrange("p l w -> p w l")
            )

        def store(hop, g, n, result):
            nc.sync.dma_start(
                out=out_rows[hop][g * P : (g + 1) * P, n * P * STEPS : (n + 1) * P * STEPS],
                in_=result[:].rearrange("p w l -> p (w l)"),
            )

        for q in range(QUADS):
            quantise_x(0, q)
        for g in range(BLOCKS):
            new_operand(x1_codes, x1_scales, g, "x1")
            for pair in range(NODE_TILES // 2):
                result_even = out_pool.tile([P, P, STEPS], F32, tag="result")
                result_odd = out_pool.tile([P, P, STEPS], F32, tag="result")
                for q in range(QUADS):
                    turn = pair * QUADS + q
                    for l in range(turn * STEPS // TURNS, (turn + 1) * STEPS // TURNS):
                        node_major_bank(g, l)
                    series_major_bank(result_even, x_codes[g], x_scales[g], 2 * pair, q)
                    series_major_bank(result_odd, x_codes[g], x_scales[g], 2 * pair + 1, q)
                store(0, g, 2 * pair, result_even)
                store(0, g, 2 * pair + 1, result_odd)
            for pair in range(NODE_TILES // 2):
                result_even = out_pool.tile([P, P, STEPS], F32, tag="result")
                result_odd = out_pool.tile([P, P, STEPS], F32, tag="result")
                for q in range(QUADS):
                    turn = pair * QUADS + q
                    if g + 1 < BLOCKS and turn % 2 == 0:
                        quantise_x(g + 1, turn // 2)
                    series_major_bank(result_even, x1_codes[g], x1_scales[g], 2 * pair, q)
                    series_major_bank(result_odd, x1_codes[g], x1_scales[g], 2 * pair + 1, q)
                store(1, g, 2 * pair, result_even)
                store(1, g, 2 * pair + 1, result_odd)
